import numpy as np
import ml_dtypes


def mxq(x, axis, fmt="e4m3"):
    dtype, down = {"e4m3": (ml_dtypes.float8_e4m3fn, 7), "e5m2": (ml_dtypes.float8_e5m2, 14)}[fmt]
    v = np.moveaxis(np.asarray(x, np.float32).astype(ml_dtypes.bfloat16).astype(np.float64), axis, -1)
    blocks = v.reshape(v.shape[:-1] + (-1, 32))
    amax = np.abs(blocks).max(-1, keepdims=True)
    byte = np.maximum(np.where(amax > 0, np.frexp(amax)[1] - 1 + 127, 0) - down, 1)
    scale = np.exp2(byte - 127.0)
    codes = (blocks / scale).astype(np.float32).astype(dtype).astype(np.float64)
    return np.moveaxis((codes * scale).reshape(v.shape), -1, axis)


WIDE = False


def mx_kscale(k):
    if not WIDE:
        return np.ones(k)
    levels = np.array([10, -10, 5, -5, 0])
    if k % 512:
        return np.exp2(np.random.permutation(np.resize(levels, k // 32))).repeat(32)
    a = np.empty((k // 512, 16))
    for p in range(k // 512):
        a[p, :8] = np.random.permutation(np.resize(levels, 8))
        for g in range(8):
            far = levels[np.abs(levels - a[p, g]) >= 10]
            a[p, g + 8] = far[np.random.randint(len(far))]
    return np.exp2(a.ravel()).repeat(32)


BF16 = ml_dtypes.bfloat16


def bf(x):
    return np.asarray(x, np.float32).astype(BF16)


def f64(x):
    return np.asarray(x).astype(np.float64)


B, N, HID, ITERS = 512, 32, 2048, 10
DIN = 2 * N * N
SLOPE = 0.01


def leaky(v):
    return np.where(v >= 0.0, v, SLOPE * v)


def setup_inputs():
    s, t = mx_kscale(DIN), mx_kscale(HID)
    sp, sq = s[0::2].reshape(N, N), s[1::2].reshape(N, N)
    return {"p": bf(np.random.uniform(size=(B, N, N)) * sp),
            "q": bf(np.random.uniform(size=(B, N, N)) * sq),
            "W1": bf(np.random.standard_normal((DIN, HID)) * 1.7 / np.sqrt(DIN) / s[:, None] * t),
            "b1": bf(np.random.standard_normal(HID) * 0.3 * t),
            "W2": bf(np.random.standard_normal((HID, HID)) * 1.4 / np.sqrt(HID) / t[:, None]),
            "b2": bf(np.random.standard_normal(HID) * 0.3)}


def reference(p, q, W1, b1, W2, b2):
    x = np.stack([f64(p), f64(q)], axis=-1).reshape(B, DIN)
    h1 = leaky((mxq(x, 1, "e4m3") @ mxq(f64(W1), 0, "e4m3")) + f64(b1))
    return leaky((mxq(h1, 1, "e4m3") @ mxq(f64(W2), 0, "e4m3")) + f64(b2))

@@ -1,0 +1,277 @@
+from contextlib import ExitStack
+
+import concourse.mybir as mybir
+from concourse.masks import make_identity
+
+F32 = mybir.dt.float32
+BF16 = mybir.dt.bfloat16
+U32 = mybir.dt.uint32
+U8 = mybir.dt.uint8
+FP8X4 = mybir.dt.float8_e4m3fn_x4
+ALU = mybir.AluOpType
+ACT = mybir.ActivationFunctionType
+
+P = 128
+PACK = 4
+K_PASS = P * PACK
+BATCH = 512
+WIDTH = 2048
+SLOPE = 0.01
+PASSES = WIDTH // K_PASS
+SAMPLE_TILES = BATCH // P
+
+BLOCK_COLS = 512
+BLOCKS = WIDTH // BLOCK_COLS
+BLOCK_BANKS = 4
+CHUNK_PASSES = 2
+CHUNK_ROWS = CHUNK_PASSES * K_PASS
+BLOCK_CHUNKS = PASSES // CHUNK_PASSES
+LAYER_CHUNKS = BLOCKS * BLOCK_CHUNKS
+CHUNKS = 2 * LAYER_CHUNKS
+
+RAW_BUFS = 10
+RUN = 4
+
+VECTOR_COLS = 256
+VECTOR_CHUNKS = 11
+
+QUANTISE_LAG = 1
+MULTIPLY_LAG = 2
+BIAS_LAG = 2
+LEAKY_LAG = 3
+REQUANTISE_LAG = 4
+FINISH_LAG = 2
+
+FLOPS = 2 * 2 * BATCH * WIDTH * WIDTH
+
+
+def tile_matchingnet_pb_kernel(tc, p, q, W1, b1, W2, b2, out):
+    nc = tc.nc
+    with ExitStack() as ctx:
+        keep = ctx.enter_context(tc.tile_pool(name="keep", bufs=1))
+        raw_pool = ctx.enter_context(tc.tile_pool(name="raw", bufs=RAW_BUFS))
+        grouped_pool = ctx.enter_context(tc.tile_pool(name="grouped", bufs=4))
+        weight_pool = ctx.enter_context(tc.tile_pool(name="weight", bufs=4))
+        hidden_pool = ctx.enter_context(tc.tile_pool(name="hidden", bufs=2))
+        result_pool = ctx.enter_context(tc.tile_pool(name="result", bufs=3))
+        psum = ctx.enter_context(tc.psum_pool(name="psum", bufs=8))
+
+        raw_of = {}
+        grouped_of = {}
+        codes_of = {}
+        scales_of = {}
+        banks_of = {}
+        biased_of = {}
+        hidden_of = {}
+        biased_out_of = {}
+
+        x_codes = keep.tile([P, PASSES, BATCH], U32, align_bytes=64)
+        x_scales = keep.tile([P, PASSES, BATCH], U8, align_bytes=64)
+        h_codes = keep.tile([P, PASSES, BATCH], U32, align_bytes=64)
+        h_scales = keep.tile([P, PASSES, BATCH], U8, align_bytes=64)
+        p_rows = keep.tile([P, SAMPLE_TILES * WIDTH // 2], BF16)
+        q_rows = keep.tile([P, SAMPLE_TILES * WIDTH // 2], BF16)
+        b1_cols = keep.tile([P, BLOCKS, PACK], BF16)
+        b2_all = keep.tile([P, WIDTH], BF16)
+        ident_f32 = keep.tile([P, P], F32)
+
+        def place(chunk):
+            layer, rest = divmod(chunk, LAYER_CHUNKS)
+            block, half = divmod(rest, BLOCK_CHUNKS)
+            return layer, block, half
+
+        def load_weights(chunk):
+            layer, block, half = place(chunk)
+            rows = slice(half * CHUNK_ROWS, (half + 1) * CHUNK_ROWS)
+            cols = slice(block * BLOCK_COLS, (block + 1) * BLOCK_COLS)
+            raw = raw_pool.tile([P, CHUNK_PASSES, PACK, BLOCK_COLS], BF16)
+            if layer == 0:
+                by_table = W1[rows, cols].rearrange(
+                    "(c r u e) w -> c e r u w", c=CHUNK_PASSES, u=2, e=2
+                )
+                for c in range(CHUNK_PASSES):
+                    for e in range(2):
+                        nc.sync.dma_start(out=raw[:, c, 2 * e : 2 * e + 2, :], in_=by_table[c, e])
+            else:
+                by_pass = W2[rows, cols].rearrange("(c r t) w -> c r t w", c=CHUNK_PASSES, r=P)
+                for c in range(CHUNK_PASSES):
+                    nc.sync.dma_start(out=raw[:, c, :, :], in_=by_pass[c])
+            raw_of[chunk] = raw
+
+        def regroup(chunk):
+            layer = place(chunk)[0]
+            split = (VECTOR_COLS if chunk < VECTOR_CHUNKS else 0) // RUN
+            raw = raw_of[chunk]
+            grouped = grouped_pool.tile([P, CHUNK_PASSES, BLOCK_COLS, PACK], BF16, align_bytes=64)
+            src = raw[:].rearrange("r c t (w i) -> r c w t i", i=RUN)
+            if layer == 0:
+                dst = grouped[:].rearrange("r c (i w) t -> r c w t i", i=RUN)
+            else:
+                dst = grouped[:].rearrange("r c (w i) t -> r c w t i", i=RUN)
+            if split > 0:
+                nc.vector.tensor_copy(out=dst[:, :, :split, :, :], in_=src[:, :, :split, :, :])
+            for c in range(CHUNK_PASSES):
+                nc.scalar.copy(out=dst[:, c, split:, :, :], in_=src[:, c, split:, :, :])
+            grouped_of[chunk] = grouped
+
+        def quantise_weights(chunk):
+            codes = weight_pool.tile([P, CHUNK_PASSES * BLOCK_COLS], U32, align_bytes=64)
+            scales = weight_pool.tile([P, CHUNK_PASSES * BLOCK_COLS], U8, align_bytes=64)
+            nc.vector.quantize_mx(
+                out=codes[:].bitcast(FP8X4),
+                scales=scales[:],
+                in_=grouped_of[chunk][:].rearrange("r c w t -> r (c w t)"),
+            )
+            codes_of[chunk] = codes
+            scales_of[chunk] = scales
+
+        def multiply(chunk):
+            layer, block, half = place(chunk)
+            if half == 0:
+                banks_of[layer, block] = [
+                    psum.tile([P, BLOCK_COLS], F32, tag="bank", name="acc%d" % b)
+                    for b in range(BLOCK_BANKS)
+                ]
+            codes = codes_of[chunk]
+            scales = scales_of[chunk]
+            for b in range(BLOCK_BANKS):
+                tile_cols = slice(b * P, (b + 1) * P)
+                for c in range(CHUNK_PASSES):
+                    k_pass = half * CHUNK_PASSES + c
+                    first = c * BLOCK_COLS
+                    if layer == 0:
+                        units = slice(first + b * P, first + (b + 1) * P)
+                        lhsT, lhsT_scale = codes[:, units], scales[:, units]
+                        rhs, rhs_scale = x_codes[:, k_pass, :], x_scales[:, k_pass, :]
+                    else:
+                        lhsT, lhsT_scale = h_codes[:, k_pass, tile_cols], h_scales[:, k_pass, tile_cols]
+                        columns = slice(first, first + BLOCK_COLS)
+                        rhs, rhs_scale = codes[:, columns], scales[:, columns]
+                    nc.tensor.matmul_mx(
+                        out=banks_of[layer, block][b][:],
+                        lhsT=lhsT.bitcast(FP8X4),
+                        lhsT_scale=lhsT_scale,
+                        rhs=rhs.bitcast(FP8X4),
+                        rhs_scale=rhs_scale,
+                        start=(k_pass == 0),
+                        stop=(k_pass == PASSES - 1),
+                    )
+
+        def prepare_inputs():
+            words_of_table = (p_rows[:].bitcast(F32), q_rows[:].bitcast(F32))
+            sample_words = WIDTH // 4
+            grouped_x = {}
+            for k_pass in range(PASSES + 1):
+                if k_pass < PASSES:
+                    x_tile = hidden_pool.tile([P, BATCH * PACK], BF16, tag="x", align_bytes=64)
+                    x_words = x_tile[:].bitcast(F32).rearrange("r (n e) -> r n e", e=2)
+                    for pair in range(SAMPLE_TILES // 2):
+                        bank = psum.tile([P, 2, 2 * P], F32, tag="bank")
+                        for e in range(2):
+                            for s in range(2):
+                                first = (2 * pair + s) * sample_words + k_pass * P
+                                nc.tensor.transpose(
+                                    bank[:, e, s * P : (s + 1) * P],
+                                    words_of_table[e][:, first : first + P],
+                                    ident_f32[:],
+                                )
+                        nc.scalar.copy(
+                            out=x_words[:, pair * 2 * P : (pair + 1) * 2 * P, :],
+                            in_=bank[:].rearrange("r e n -> r n e"),
+                        )
+                    grouped_x[k_pass] = x_tile
+                if k_pass > 0:
+                    nc.vector.quantize_mx(
+                        out=x_codes[:, k_pass - 1, :].bitcast(FP8X4),
+                        scales=x_scales[:, k_pass - 1, :],
+                        in_=grouped_x[k_pass - 1][:],
+                    )
+
+        def add_hidden_bias(block):
+            biased = hidden_pool.tile([P, PACK, BATCH], F32)
+            for t in range(PACK):
+                nc.scalar.activation(
+                    out=biased[:, t, :],
+                    in_=banks_of[0, block][t][:],
+                    func=ACT.Identity,
+                    bias=b1_cols[:, block, t : t + 1],
+                    scale=1.0,
+                )
+            biased_of[block] = biased
+
+        def leaky_hidden(block):
+            hidden = hidden_pool.tile([P, BATCH, PACK], BF16, align_bytes=64)
+            by_sample = biased_of[block][:].rearrange("r t n -> r n t")
+            nc.vector.scalar_tensor_tensor(
+                out=hidden[:], in0=by_sample, scalar=SLOPE, in1=by_sample, op0=ALU.mult, op1=ALU.max
+            )
+            hidden_of[block] = hidden
+
+        def quantise_hidden(block):
+            nc.vector.quantize_mx(
+                out=h_codes[:, block, :].bitcast(FP8X4),
+                scales=h_scales[:, block, :],
+                in_=hidden_of[block][:].rearrange("r n t -> r (n t)"),
+            )
+
+        def add_output_bias(block, first_tile):
+            cols = slice(block * BLOCK_COLS, (block + 1) * BLOCK_COLS)
+            biased = result_pool.tile([P, 2, BLOCK_COLS], F32, tag="biased_out")
+            for s in range(2):
+                nc.vector.tensor_tensor(
+                    out=biased[:, s, :],
+                    in0=banks_of[1, block][first_tile + s][:],
+                    in1=b2_all[:, cols],
+                    op=ALU.add,
+                )
+            biased_out_of[block, first_tile] = biased
+
+        def leaky_output(block, first_tile):
+            cols = slice(block * BLOCK_COLS, (block + 1) * BLOCK_COLS)
+            biased = biased_out_of[block, first_tile]
+            result = result_pool.tile([P, 2, BLOCK_COLS], F32)
+            nc.vector.scalar_tensor_tensor(
+                out=result[:], in0=biased[:], scalar=SLOPE, in1=biased[:], op0=ALU.mult, op1=ALU.max
+            )
+            rows = out.rearrange("(r s) j -> r s j", s=SAMPLE_TILES)
+            nc.sync.dma_start(out=rows[:, first_tile : first_tile + 2, cols], in_=result[:])
+
+        make_identity(nc, ident_f32[:])
+        nc.scalar.dma_start(out=b1_cols[:], in_=b1.rearrange("(b p t) -> p b t", b=BLOCKS, t=PACK))
+        load_weights(0)
+        nc.sync.dma_start(out=p_rows[:], in_=p.rearrange("(r s) i j -> r (s i j)", s=SAMPLE_TILES))
+        nc.sync.dma_start(out=q_rows[:], in_=q.rearrange("(r s) i j -> r (s i j)", s=SAMPLE_TILES))
+        for chunk in range(1, RAW_BUFS):
+            load_weights(chunk)
+        nc.sync.dma_start(out=b2_all[:], in_=b2.partition_broadcast(P))
+
+        def completed(step, lag, layer):
+            chunk = step - lag
+            if 0 <= chunk < CHUNKS and chunk % BLOCK_CHUNKS == BLOCK_CHUNKS - 1:
+                if place(chunk)[0] == layer:
+                    return place(chunk)[1]
+            return None
+
+        for step in range(CHUNKS + FINISH_LAG + 2):
+            if step < CHUNKS:
+                regroup(step)
+            if step + RAW_BUFS < CHUNKS:
+                load_weights(step + RAW_BUFS)
+            if step == 0:
+                prepare_inputs()
+            if completed(step, REQUANTISE_LAG, 0) is not None:
+                quantise_hidden(completed(step, REQUANTISE_LAG, 0))
+            if 0 <= step - QUANTISE_LAG < CHUNKS:
+                quantise_weights(step - QUANTISE_LAG)
+            if 0 <= step - MULTIPLY_LAG < CHUNKS:
+                multiply(step - MULTIPLY_LAG)
+            if completed(step, BIAS_LAG, 0) is not None:
+                add_hidden_bias(completed(step, BIAS_LAG, 0))
+            if completed(step, LEAKY_LAG, 0) is not None:
+                leaky_hidden(completed(step, LEAKY_LAG, 0))
+            for half_lag, first_tile in ((0, 0), (1, 2)):
+                if completed(step, FINISH_LAG + half_lag, 1) is not None:
+                    add_output_bias(completed(step, FINISH_LAG + half_lag, 1), first_tile)
+            for half_lag, first_tile in ((0, 0), (1, 2)):
+                if completed(step, FINISH_LAG + half_lag + 1, 1) is not None:
+                    leaky_output(completed(step, FINISH_LAG + half_lag + 1, 1), first_tile)

@@ -21,18 +21,17 @@ PASSES = WIDTH // K_PASS
 SAMPLE_TILES = BATCH // P
 
 BLOCK_COLS = 512
-BLOCKS = WIDTH // BLOCK_COLS
-BLOCK_BANKS = 4
-CHUNK_PASSES = 2
-CHUNK_ROWS = CHUNK_PASSES * K_PASS
-BLOCK_CHUNKS = PASSES // CHUNK_PASSES
-LAYER_CHUNKS = BLOCKS * BLOCK_CHUNKS
-CHUNKS = 2 * LAYER_CHUNKS
+LAST_COLS = 256
+BANKS = 4
+LOAD_PASSES = 2
+LOAD_ROWS = LOAD_PASSES * K_PASS
+LAYER_LOADS = (PASSES // LOAD_PASSES) * (WIDTH // BLOCK_COLS)
+LOADS = 2 * LAYER_LOADS
+CHUNK_WORDS = LOAD_PASSES * BLOCK_COLS
 
 RAW_BUFS = 10
 RUN = 4
 
-VECTOR_COLS = 256
 VECTOR_CHUNKS = 11
 
 QUANTISE_LAG = 1
@@ -45,17 +44,35 @@ FINISH_LAG = 2
 FLOPS = 2 * 2 * BATCH * WIDTH * WIDTH
 
 
+def plan_chunks():
+    chunks = []
+    for layer in range(2):
+        for block in range(WIDTH // BLOCK_COLS):
+            first_load = layer * LAYER_LOADS + block * 2
+            start = block * BLOCK_COLS
+            if (layer, block) == (1, WIDTH // BLOCK_COLS - 1):
+                for half in range(2):
+                    first = start + half * LAST_COLS
+                    chunks.append((1, block + half, first, LAST_COLS, range(4), (first_load, first_load + 1)))
+            else:
+                chunks.append((layer, block, start, BLOCK_COLS, range(0, 2), (first_load,)))
+                chunks.append((layer, block, start, BLOCK_COLS, range(2, 4), (first_load + 1,)))
+    return chunks
+
+
 def tile_matchingnet_pb_kernel(tc, p, q, W1, b1, W2, b2, out):
     nc = tc.nc
+    chunks = plan_chunks()
     with ExitStack() as ctx:
         keep = ctx.enter_context(tc.tile_pool(name="keep", bufs=1))
         raw_pool = ctx.enter_context(tc.tile_pool(name="raw", bufs=RAW_BUFS))
         grouped_pool = ctx.enter_context(tc.tile_pool(name="grouped", bufs=4))
         weight_pool = ctx.enter_context(tc.tile_pool(name="weight", bufs=4))
         hidden_pool = ctx.enter_context(tc.tile_pool(name="hidden", bufs=2))
-        result_pool = ctx.enter_context(tc.tile_pool(name="result", bufs=3))
+        result_pool = ctx.enter_context(tc.tile_pool(name="result", bufs=6))
         psum = ctx.enter_context(tc.psum_pool(name="psum", bufs=8))
 
+        x_rows_of = {}
         raw_of = {}
         grouped_of = {}
         codes_of = {}
@@ -63,92 +80,94 @@ def tile_matchingnet_pb_kernel(tc, p, q, W1, b1, W2, b2, out):
         banks_of = {}
         biased_of = {}
         hidden_of = {}
-        biased_out_of = {}
+        result_of = {}
 
         x_codes = keep.tile([P, PASSES, BATCH], U32, align_bytes=64)
         x_scales = keep.tile([P, PASSES, BATCH], U8, align_bytes=64)
         h_codes = keep.tile([P, PASSES, BATCH], U32, align_bytes=64)
         h_scales = keep.tile([P, PASSES, BATCH], U8, align_bytes=64)
-        p_rows = keep.tile([P, SAMPLE_TILES * WIDTH // 2], BF16)
-        q_rows = keep.tile([P, SAMPLE_TILES * WIDTH // 2], BF16)
-        b1_cols = keep.tile([P, BLOCKS, PACK], BF16)
+        b1_cols = keep.tile([P, WIDTH // BLOCK_COLS, PACK], BF16)
         b2_all = keep.tile([P, WIDTH], BF16)
         ident_f32 = keep.tile([P, P], F32)
+        one = keep.tile([P, 1], F32)
+        loaded = keep.tile([P, 1], F32)
 
-        def place(chunk):
-            layer, rest = divmod(chunk, LAYER_CHUNKS)
-            block, half = divmod(rest, BLOCK_CHUNKS)
-            return layer, block, half
-
-        def load_weights(chunk):
-            layer, block, half = place(chunk)
-            rows = slice(half * CHUNK_ROWS, (half + 1) * CHUNK_ROWS)
+        def load_weights(load):
+            layer, rest = divmod(load, LAYER_LOADS)
+            block, half = divmod(rest, 2)
+            rows = slice(half * LOAD_ROWS, (half + 1) * LOAD_ROWS)
             cols = slice(block * BLOCK_COLS, (block + 1) * BLOCK_COLS)
-            raw = raw_pool.tile([P, CHUNK_PASSES, PACK, BLOCK_COLS], BF16)
+            raw = raw_pool.tile([P, LOAD_PASSES, PACK, BLOCK_COLS], BF16)
             if layer == 0:
                 by_table = W1[rows, cols].rearrange(
-                    "(c r u e) w -> c e r u w", c=CHUNK_PASSES, u=2, e=2
+                    "(c r u e) w -> c e r u w", c=LOAD_PASSES, u=2, e=2
                 )
-                for c in range(CHUNK_PASSES):
+                for c in range(LOAD_PASSES):
                     for e in range(2):
                         nc.sync.dma_start(out=raw[:, c, 2 * e : 2 * e + 2, :], in_=by_table[c, e])
             else:
-                by_pass = W2[rows, cols].rearrange("(c r t) w -> c r t w", c=CHUNK_PASSES, r=P)
-                for c in range(CHUNK_PASSES):
+                by_pass = W2[rows, cols].rearrange("(c r t) w -> c r t w", c=LOAD_PASSES, r=P)
+                for c in range(LOAD_PASSES):
                     nc.sync.dma_start(out=raw[:, c, :, :], in_=by_pass[c])
-            raw_of[chunk] = raw
+            raw_of[load] = raw
+
+        def load_inputs(half):
+            words = slice(half * WIDTH // 4, (half + 1) * WIDTH // 4)
+            for name, table in (("p", p), ("q", q)):
+                rows = keep.tile([P, SAMPLE_TILES, WIDTH // 4], BF16, name="%s_rows%d" % (name, half))
+                by_sample = table.rearrange("(r s) i j -> r s (i j)", s=SAMPLE_TILES)
+                nc.sync.dma_start(out=rows[:], in_=by_sample[:, :, words])
+                x_rows_of[name, half] = rows
 
         def regroup(chunk):
-            layer = place(chunk)[0]
-            split = (VECTOR_COLS if chunk < VECTOR_CHUNKS else 0) // RUN
-            raw = raw_of[chunk]
-            grouped = grouped_pool.tile([P, CHUNK_PASSES, BLOCK_COLS, PACK], BF16, align_bytes=64)
-            src = raw[:].rearrange("r c t (w i) -> r c w t i", i=RUN)
-            if layer == 0:
-                dst = grouped[:].rearrange("r c (i w) t -> r c w t i", i=RUN)
-            else:
-                dst = grouped[:].rearrange("r c (w i) t -> r c w t i", i=RUN)
-            if split > 0:
-                nc.vector.tensor_copy(out=dst[:, :, :split, :, :], in_=src[:, :, :split, :, :])
-            for c in range(CHUNK_PASSES):
-                nc.scalar.copy(out=dst[:, c, split:, :, :], in_=src[:, c, split:, :, :])
+            layer, block, first_col, width, passes, loads = chunks[chunk]
+            grouped = grouped_pool.tile([P, CHUNK_WORDS * PACK], BF16, align_bytes=64)
             grouped_of[chunk] = grouped
+            order = "r (c i w t) -> r c w t i" if layer == 0 else "r (c w i t) -> r c w t i"
+            dst = grouped[:].rearrange(order, c=len(passes), i=RUN, t=PACK)
+            split = (width // 2 if chunk < VECTOR_CHUNKS else 0) // RUN
+            offset = first_col % BLOCK_COLS
+            for n, load in enumerate(loads):
+                src = raw_of[load][:, :, :, offset : offset + width].rearrange("r c t (w i) -> r c w t i", i=RUN)
+                part = dst[:, n * LOAD_PASSES : (n + 1) * LOAD_PASSES]
+                if split > 0:
+                    if chunk == 0:
+                        for c in range(LOAD_PASSES):
+                            nc.vector.tensor_copy(out=part[:, c, :split], in_=src[:, c, :split])
+                    else:
+                        nc.vector.tensor_copy(out=part[:, :, :split], in_=src[:, :, :split])
+                for c in range(LOAD_PASSES):
+                    nc.scalar.copy(out=part[:, c, split:], in_=src[:, c, split:])
 
         def quantise_weights(chunk):
-            codes = weight_pool.tile([P, CHUNK_PASSES * BLOCK_COLS], U32, align_bytes=64)
-            scales = weight_pool.tile([P, CHUNK_PASSES * BLOCK_COLS], U8, align_bytes=64)
-            nc.vector.quantize_mx(
-                out=codes[:].bitcast(FP8X4),
-                scales=scales[:],
-                in_=grouped_of[chunk][:].rearrange("r c w t -> r (c w t)"),
-            )
+            codes = weight_pool.tile([P, CHUNK_WORDS], U32, align_bytes=64)
+            scales = weight_pool.tile([P, CHUNK_WORDS], U8, align_bytes=64)
+            nc.vector.quantize_mx(out=codes[:].bitcast(FP8X4), scales=scales[:], in_=grouped_of[chunk][:])
             codes_of[chunk] = codes
             scales_of[chunk] = scales
 
         def multiply(chunk):
-            layer, block, half = place(chunk)
-            if half == 0:
+            layer, block, first_col, width, passes, loads = chunks[chunk]
+            if passes[0] == 0:
                 banks_of[layer, block] = [
-                    psum.tile([P, BLOCK_COLS], F32, tag="bank", name="acc%d" % b)
-                    for b in range(BLOCK_BANKS)
+                    psum.tile([P, BLOCK_COLS], F32, tag="bank", name="acc%d" % b) for b in range(BANKS)
                 ]
             codes = codes_of[chunk]
             scales = scales_of[chunk]
-            for b in range(BLOCK_BANKS):
+            for b in range(BANKS):
                 tile_cols = slice(b * P, (b + 1) * P)
-                for c in range(CHUNK_PASSES):
-                    k_pass = half * CHUNK_PASSES + c
-                    first = c * BLOCK_COLS
+                for c, k_pass in enumerate(passes):
+                    first = c * width
                     if layer == 0:
                         units = slice(first + b * P, first + (b + 1) * P)
                         lhsT, lhsT_scale = codes[:, units], scales[:, units]
                         rhs, rhs_scale = x_codes[:, k_pass, :], x_scales[:, k_pass, :]
                     else:
                         lhsT, lhsT_scale = h_codes[:, k_pass, tile_cols], h_scales[:, k_pass, tile_cols]
-                        columns = slice(first, first + BLOCK_COLS)
+                        columns = slice(first, first + width)
                         rhs, rhs_scale = codes[:, columns], scales[:, columns]
                     nc.tensor.matmul_mx(
-                        out=banks_of[layer, block][b][:],
+                        out=banks_of[layer, block][b][:, : BATCH if layer == 0 else width],
                         lhsT=lhsT.bitcast(FP8X4),
                         lhsT_scale=lhsT_scale,
                         rhs=rhs.bitcast(FP8X4),
@@ -157,35 +176,33 @@ def tile_matchingnet_pb_kernel(tc, p, q, W1, b1, W2, b2, out):
                         stop=(k_pass == PASSES - 1),
                     )
 
-        def prepare_inputs():
-            words_of_table = (p_rows[:].bitcast(F32), q_rows[:].bitcast(F32))
-            sample_words = WIDTH // 4
+        def prepare_inputs(half):
+            words_of_table = [x_rows_of[name, half][:].bitcast(F32) for name in ("p", "q")]
             grouped_x = {}
-            for k_pass in range(PASSES + 1):
-                if k_pass < PASSES:
-                    x_tile = hidden_pool.tile([P, BATCH * PACK], BF16, tag="x", align_bytes=64)
-                    x_words = x_tile[:].bitcast(F32).rearrange("r (n e) -> r n e", e=2)
-                    for pair in range(SAMPLE_TILES // 2):
-                        bank = psum.tile([P, 2, 2 * P], F32, tag="bank")
-                        for e in range(2):
-                            for s in range(2):
-                                first = (2 * pair + s) * sample_words + k_pass * P
-                                nc.tensor.transpose(
-                                    bank[:, e, s * P : (s + 1) * P],
-                                    words_of_table[e][:, first : first + P],
-                                    ident_f32[:],
-                                )
-                        nc.scalar.copy(
-                            out=x_words[:, pair * 2 * P : (pair + 1) * 2 * P, :],
-                            in_=bank[:].rearrange("r e n -> r n e"),
-                        )
-                    grouped_x[k_pass] = x_tile
-                if k_pass > 0:
-                    nc.vector.quantize_mx(
-                        out=x_codes[:, k_pass - 1, :].bitcast(FP8X4),
-                        scales=x_scales[:, k_pass - 1, :],
-                        in_=grouped_x[k_pass - 1][:],
+            for c in range(2):
+                k_pass = 2 * half + c
+                x_tile = hidden_pool.tile([P, BATCH * PACK], BF16, tag="x", align_bytes=64)
+                x_words = x_tile[:].bitcast(F32).rearrange("r (n e) -> r n e", e=2)
+                for pair in range(SAMPLE_TILES // 2):
+                    bank = psum.tile([P, 2, 2 * P], F32, tag="bank")
+                    for e in range(2):
+                        for s in range(2):
+                            nc.tensor.transpose(
+                                bank[:, e, s * P : (s + 1) * P],
+                                words_of_table[e][:, 2 * pair + s, c * P : (c + 1) * P],
+                                ident_f32[:],
+                            )
+                    nc.scalar.copy(
+                        out=x_words[:, pair * 2 * P : (pair + 1) * 2 * P, :],
+                        in_=bank[:].rearrange("r e n -> r n e"),
                     )
+                grouped_x[k_pass] = x_tile
+            for k_pass in (2 * half, 2 * half + 1):
+                nc.vector.quantize_mx(
+                    out=x_codes[:, k_pass, :].bitcast(FP8X4),
+                    scales=x_scales[:, k_pass, :],
+                    in_=grouped_x[k_pass][:],
+                )
 
         def add_hidden_bias(block):
             biased = hidden_pool.tile([P, PACK, BATCH], F32)
@@ -214,61 +231,67 @@ def tile_matchingnet_pb_kernel(tc, p, q, W1, b1, W2, b2, out):
                 in_=hidden_of[block][:].rearrange("r n t -> r (n t)"),
             )
 
-        def add_output_bias(block, first_tile):
-            cols = slice(block * BLOCK_COLS, (block + 1) * BLOCK_COLS)
-            biased = result_pool.tile([P, 2, BLOCK_COLS], F32, tag="biased_out")
+        def add_output_bias(chunk, first_tile):
+            layer, block, first_col, width, passes, loads = chunks[chunk]
+            result = result_pool.tile([P, 2, width], F32, tag="result")
             for s in range(2):
                 nc.vector.tensor_tensor(
-                    out=biased[:, s, :],
-                    in0=banks_of[1, block][first_tile + s][:],
-                    in1=b2_all[:, cols],
+                    out=result[:, s, :],
+                    in0=banks_of[1, block][first_tile + s][:, :width],
+                    in1=b2_all[:, first_col : first_col + width],
                     op=ALU.add,
                 )
-            biased_out_of[block, first_tile] = biased
+            result_of[chunk, first_tile] = result
 
-        def leaky_output(block, first_tile):
-            cols = slice(block * BLOCK_COLS, (block + 1) * BLOCK_COLS)
-            biased = biased_out_of[block, first_tile]
-            result = result_pool.tile([P, 2, BLOCK_COLS], F32)
+        def leaky_output(chunk, first_tile):
+            layer, block, first_col, width, passes, loads = chunks[chunk]
+            result = result_of[chunk, first_tile]
             nc.vector.scalar_tensor_tensor(
-                out=result[:], in0=biased[:], scalar=SLOPE, in1=biased[:], op0=ALU.mult, op1=ALU.max
+                out=result[:], in0=result[:], scalar=SLOPE, in1=result[:], op0=ALU.mult, op1=ALU.max
             )
             rows = out.rearrange("(r s) j -> r s j", s=SAMPLE_TILES)
-            nc.sync.dma_start(out=rows[:, first_tile : first_tile + 2, cols], in_=result[:])
+            nc.sync.dma_start(
+                out=rows[:, first_tile : first_tile + 2, first_col : first_col + width], in_=result[:]
+            )
 
+        nc.vector.memset(one[:], 1.0)
+        nc.scalar.activation(out=loaded[:], in_=one[:], func=ACT.Identity)
         make_identity(nc, ident_f32[:])
-        nc.scalar.dma_start(out=b1_cols[:], in_=b1.rearrange("(b p t) -> p b t", b=BLOCKS, t=PACK))
+        nc.scalar.dma_start(out=b1_cols[:], in_=b1.rearrange("(b p t) -> p b t", p=P, t=PACK))
         load_weights(0)
-        nc.sync.dma_start(out=p_rows[:], in_=p.rearrange("(r s) i j -> r (s i j)", s=SAMPLE_TILES))
-        nc.sync.dma_start(out=q_rows[:], in_=q.rearrange("(r s) i j -> r (s i j)", s=SAMPLE_TILES))
-        for chunk in range(1, RAW_BUFS):
-            load_weights(chunk)
+        load_inputs(0)
+        load_weights(1)
+        load_inputs(1)
+        for load in range(2, RAW_BUFS):
+            load_weights(load)
         nc.sync.dma_start(out=b2_all[:], in_=b2.partition_broadcast(P))
 
         def completed(step, lag, layer):
             chunk = step - lag
-            if 0 <= chunk < CHUNKS and chunk % BLOCK_CHUNKS == BLOCK_CHUNKS - 1:
-                if place(chunk)[0] == layer:
-                    return place(chunk)[1]
+            if 0 <= chunk < len(chunks) and chunks[chunk][0] == layer and chunks[chunk][4][-1] == PASSES - 1:
+                return chunk
             return None
 
-        for step in range(CHUNKS + FINISH_LAG + 2):
-            if step < CHUNKS:
+        def block_of(chunk):
+            return chunks[chunk][1]
+
+        for step in range(len(chunks) + FINISH_LAG + 2):
+            if step < len(chunks):
                 regroup(step)
-            if step + RAW_BUFS < CHUNKS:
+            if step + RAW_BUFS < LOADS:
                 load_weights(step + RAW_BUFS)
-            if step == 0:
-                prepare_inputs()
+            if step < 2:
+                prepare_inputs(step)
             if completed(step, REQUANTISE_LAG, 0) is not None:
-                quantise_hidden(completed(step, REQUANTISE_LAG, 0))
-            if 0 <= step - QUANTISE_LAG < CHUNKS:
+                quantise_hidden(block_of(completed(step, REQUANTISE_LAG, 0)))
+            if 0 <= step - QUANTISE_LAG < len(chunks):
                 quantise_weights(step - QUANTISE_LAG)
-            if 0 <= step - MULTIPLY_LAG < CHUNKS:
+            if 0 <= step - MULTIPLY_LAG < len(chunks):
                 multiply(step - MULTIPLY_LAG)
             if completed(step, BIAS_LAG, 0) is not None:
-                add_hidden_bias(completed(step, BIAS_LAG, 0))
+                add_hidden_bias(block_of(completed(step, BIAS_LAG, 0)))
             if completed(step, LEAKY_LAG, 0) is not None:
-                leaky_hidden(completed(step, LEAKY_LAG, 0))
+                leaky_hidden(block_of(completed(step, LEAKY_LAG, 0)))
             for half_lag, first_tile in ((0, 0), (1, 2)):
                 if completed(step, FINISH_LAG + half_lag, 1) is not None:
                     add_output_bias(completed(step, FINISH_LAG + half_lag, 1), first_tile)

@@ -23,11 +23,11 @@ SAMPLE_TILES = BATCH // P
 BLOCK_COLS = 512
 LAST_COLS = 256
 BANKS = 4
-LOAD_PASSES = 2
-LOAD_ROWS = LOAD_PASSES * K_PASS
-LAYER_LOADS = (PASSES // LOAD_PASSES) * (WIDTH // BLOCK_COLS)
+LOAD_COLS = 2 * BLOCK_COLS
+LAYER_LOADS = PASSES * (WIDTH // LOAD_COLS)
 LOADS = 2 * LAYER_LOADS
-CHUNK_WORDS = LOAD_PASSES * BLOCK_COLS
+NARROW_LOADS = 4
+CHUNK_WORDS = 2 * BLOCK_COLS
 
 RAW_BUFS = 10
 RUN = 4
@@ -48,15 +48,13 @@ def plan_chunks():
     chunks = []
     for layer in range(2):
         for block in range(WIDTH // BLOCK_COLS):
-            first_load = layer * LAYER_LOADS + block * 2
             start = block * BLOCK_COLS
             if (layer, block) == (1, WIDTH // BLOCK_COLS - 1):
                 for half in range(2):
-                    first = start + half * LAST_COLS
-                    chunks.append((1, block + half, first, LAST_COLS, range(4), (first_load, first_load + 1)))
+                    chunks.append((1, block + half, start + half * LAST_COLS, LAST_COLS, range(4)))
             else:
-                chunks.append((layer, block, start, BLOCK_COLS, range(0, 2), (first_load,)))
-                chunks.append((layer, block, start, BLOCK_COLS, range(2, 4), (first_load + 1,)))
+                chunks.append((layer, block, start, BLOCK_COLS, range(0, 2)))
+                chunks.append((layer, block, start, BLOCK_COLS, range(2, 4)))
     return chunks
 
 
@@ -94,22 +92,29 @@ def tile_matchingnet_pb_kernel(tc, p, q, W1, b1, W2, b2, out):
 
         def load_weights(load):
             layer, rest = divmod(load, LAYER_LOADS)
-            block, half = divmod(rest, 2)
-            rows = slice(half * LOAD_ROWS, (half + 1) * LOAD_ROWS)
-            cols = slice(block * BLOCK_COLS, (block + 1) * BLOCK_COLS)
-            raw = raw_pool.tile([P, LOAD_PASSES, PACK, BLOCK_COLS], BF16)
-            if layer == 0:
-                by_table = W1[rows, cols].rearrange(
-                    "(c r u e) w -> c e r u w", c=LOAD_PASSES, u=2, e=2
-                )
-                for c in range(LOAD_PASSES):
+            if load < NARROW_LOADS:
+                block, half = divmod(load, 2)
+                rows = slice(2 * half * K_PASS, 2 * (half + 1) * K_PASS)
+                cols = slice(block * BLOCK_COLS, (block + 1) * BLOCK_COLS)
+                raw = raw_pool.tile([P, 2, PACK, BLOCK_COLS], BF16, tag="raw")
+                by_table = W1[rows, cols].rearrange("(c r u e) w -> c e r u w", c=2, u=2, e=2)
+                for c in range(2):
                     for e in range(2):
                         nc.sync.dma_start(out=raw[:, c, 2 * e : 2 * e + 2, :], in_=by_table[c, e])
+                    raw_of[0, 2 * half + c, block] = raw[:, c]
+                return
+            part, k_pass = divmod(rest, PASSES)
+            rows = slice(k_pass * K_PASS, (k_pass + 1) * K_PASS)
+            cols = slice(part * LOAD_COLS, (part + 1) * LOAD_COLS)
+            raw = raw_pool.tile([P, PACK, LOAD_COLS], BF16, tag="raw")
+            if layer == 0:
+                by_table = W1[rows, cols].rearrange("(r u e) w -> e r u w", u=2, e=2)
+                for e in range(2):
+                    nc.sync.dma_start(out=raw[:, 2 * e : 2 * e + 2, :], in_=by_table[e])
             else:
-                by_pass = W2[rows, cols].rearrange("(c r t) w -> c r t w", c=LOAD_PASSES, r=P)
-                for c in range(LOAD_PASSES):
-                    nc.sync.dma_start(out=raw[:, c, :, :], in_=by_pass[c])
-            raw_of[load] = raw
+                nc.sync.dma_start(out=raw[:], in_=W2[rows, cols].rearrange("(r t) w -> r t w", r=P))
+            for n in range(LOAD_COLS // BLOCK_COLS):
+                raw_of[layer, k_pass, 2 * part + n] = raw[:, :, n * BLOCK_COLS : (n + 1) * BLOCK_COLS]
 
         def load_inputs(half):
             words = slice(half * WIDTH // 4, (half + 1) * WIDTH // 4)
@@ -120,24 +125,19 @@ def tile_matchingnet_pb_kernel(tc, p, q, W1, b1, W2, b2, out):
                 x_rows_of[name, half] = rows
 
         def regroup(chunk):
-            layer, block, first_col, width, passes, loads = chunks[chunk]
+            layer, block, first_col, width, passes = chunks[chunk]
             grouped = grouped_pool.tile([P, CHUNK_WORDS * PACK], BF16, align_bytes=64)
             grouped_of[chunk] = grouped
             order = "r (c i w t) -> r c w t i" if layer == 0 else "r (c w i t) -> r c w t i"
             dst = grouped[:].rearrange(order, c=len(passes), i=RUN, t=PACK)
             split = (width // 2 if chunk < VECTOR_CHUNKS else 0) // RUN
-            offset = first_col % BLOCK_COLS
-            for n, load in enumerate(loads):
-                src = raw_of[load][:, :, :, offset : offset + width].rearrange("r c t (w i) -> r c w t i", i=RUN)
-                part = dst[:, n * LOAD_PASSES : (n + 1) * LOAD_PASSES]
+            load_block, offset = divmod(first_col, BLOCK_COLS)
+            for c, k_pass in enumerate(passes):
+                raw = raw_of[layer, k_pass, load_block][:, :, offset : offset + width]
+                src = raw.rearrange("r t (w i) -> r w t i", i=RUN)
                 if split > 0:
-                    if chunk == 0:
-                        for c in range(LOAD_PASSES):
-                            nc.vector.tensor_copy(out=part[:, c, :split], in_=src[:, c, :split])
-                    else:
-                        nc.vector.tensor_copy(out=part[:, :, :split], in_=src[:, :, :split])
-                for c in range(LOAD_PASSES):
-                    nc.scalar.copy(out=part[:, c, split:], in_=src[:, c, split:])
+                    nc.vector.tensor_copy(out=dst[:, c, :split], in_=src[:, :split])
+                nc.scalar.copy(out=dst[:, c, split:], in_=src[:, split:])
 
         def quantise_weights(chunk):
             codes = weight_pool.tile([P, CHUNK_WORDS], U32, align_bytes=64)
@@ -147,7 +147,7 @@ def tile_matchingnet_pb_kernel(tc, p, q, W1, b1, W2, b2, out):
             scales_of[chunk] = scales
 
         def multiply(chunk):
-            layer, block, first_col, width, passes, loads = chunks[chunk]
+            layer, block, first_col, width, passes = chunks[chunk]
             if passes[0] == 0:
                 banks_of[layer, block] = [
                     psum.tile([P, BLOCK_COLS], F32, tag="bank", name="acc%d" % b) for b in range(BANKS)
@@ -232,7 +232,7 @@ def tile_matchingnet_pb_kernel(tc, p, q, W1, b1, W2, b2, out):
             )
 
         def add_output_bias(chunk, first_tile):
-            layer, block, first_col, width, passes, loads = chunks[chunk]
+            layer, block, first_col, width, passes = chunks[chunk]
             result = result_pool.tile([P, 2, width], F32, tag="result")
             for s in range(2):
                 nc.vector.tensor_tensor(
@@ -244,7 +244,7 @@ def tile_matchingnet_pb_kernel(tc, p, q, W1, b1, W2, b2, out):
             result_of[chunk, first_tile] = result
 
         def leaky_output(chunk, first_tile):
-            layer, block, first_col, width, passes, loads = chunks[chunk]
+            layer, block, first_col, width, passes = chunks[chunk]
             result = result_of[chunk, first_tile]
             nc.vector.scalar_tensor_tensor(
                 out=result[:], in0=result[:], scalar=SLOPE, in1=result[:], op0=ALU.mult, op1=ALU.max

@@ -38,6 +38,7 @@ QUANTISE_LAG = 1
 MULTIPLY_LAG = 2
 BIAS_LAG = 2
 LEAKY_LAG = 3
+REGROUP_LAG = 4
 REQUANTISE_LAG = 4
 FINISH_LAG = 2
 
@@ -77,6 +78,7 @@ def tile_matchingnet_pb_kernel(tc, p, q, W1, b1, W2, b2, out):
         scales_of = {}
         banks_of = {}
         biased_of = {}
+        rounded_of = {}
         hidden_of = {}
         result_of = {}
 
@@ -130,19 +132,25 @@ def tile_matchingnet_pb_kernel(tc, p, q, W1, b1, W2, b2, out):
             grouped_of[chunk] = grouped
             order = "r (c i w t) -> r c w t i" if layer == 0 else "r (c w i t) -> r c w t i"
             dst = grouped[:].rearrange(order, c=len(passes), i=RUN, t=PACK)
-            split = (width // 2 if chunk < VECTOR_CHUNKS else 0) // RUN
             load_block, offset = divmod(first_col, BLOCK_COLS)
             for c, k_pass in enumerate(passes):
                 raw = raw_of[layer, k_pass, load_block][:, :, offset : offset + width]
                 src = raw.rearrange("r t (w i) -> r w t i", i=RUN)
-                if split > 0:
-                    nc.vector.tensor_copy(out=dst[:, c, :split], in_=src[:, :split])
-                nc.scalar.copy(out=dst[:, c, split:], in_=src[:, split:])
+                if chunk < VECTOR_CHUNKS and c == 0:
+                    nc.vector.tensor_copy(out=dst[:, c], in_=src)
+                else:
+                    nc.scalar.copy(out=dst[:, c], in_=src)
 
         def quantise_weights(chunk):
             codes = weight_pool.tile([P, CHUNK_WORDS], U32, align_bytes=64)
             scales = weight_pool.tile([P, CHUNK_WORDS], U8, align_bytes=64)
-            nc.vector.quantize_mx(out=codes[:].bitcast(FP8X4), scales=scales[:], in_=grouped_of[chunk][:])
+            for half in range(2):
+                words = slice(half * CHUNK_WORDS // 2, (half + 1) * CHUNK_WORDS // 2)
+                nc.vector.quantize_mx(
+                    out=codes[:, words].bitcast(FP8X4),
+                    scales=scales[:, words],
+                    in_=grouped_of[chunk][:, PACK * words.start : PACK * words.stop],
+                )
             codes_of[chunk] = codes
             scales_of[chunk] = scales
 
@@ -217,10 +225,18 @@ def tile_matchingnet_pb_kernel(tc, p, q, W1, b1, W2, b2, out):
             biased_of[block] = biased
 
         def leaky_hidden(block):
-            hidden = hidden_pool.tile([P, BATCH, PACK], BF16, align_bytes=64)
-            by_sample = biased_of[block][:].rearrange("r t n -> r n t")
+            rounded = hidden_pool.tile([P, PACK, BATCH], BF16)
+            biased = biased_of[block]
             nc.vector.scalar_tensor_tensor(
-                out=hidden[:], in0=by_sample, scalar=SLOPE, in1=by_sample, op0=ALU.mult, op1=ALU.max
+                out=rounded[:], in0=biased[:], scalar=SLOPE, in1=biased[:], op0=ALU.mult, op1=ALU.max
+            )
+            rounded_of[block] = rounded
+
+        def regroup_hidden(block):
+            hidden = hidden_pool.tile([P, BATCH * PACK], BF16, align_bytes=64)
+            nc.vector.tensor_copy(
+                out=hidden[:].rearrange("r (n i t) -> r n t i", i=RUN, t=PACK),
+                in_=rounded_of[block][:].rearrange("r t (n i) -> r n t i", i=RUN),
             )
             hidden_of[block] = hidden
 
@@ -228,7 +244,7 @@ def tile_matchingnet_pb_kernel(tc, p, q, W1, b1, W2, b2, out):
             nc.vector.quantize_mx(
                 out=h_codes[:, block, :].bitcast(FP8X4),
                 scales=h_scales[:, block, :],
-                in_=hidden_of[block][:].rearrange("r n t -> r (n t)"),
+                in_=hidden_of[block][:],
             )
 
         def add_output_bias(chunk, first_tile):
@@ -276,16 +292,18 @@ def tile_matchingnet_pb_kernel(tc, p, q, W1, b1, W2, b2, out):
             return chunks[chunk][1]
 
         for step in range(len(chunks) + FINISH_LAG + 2):
+            if completed(step, REGROUP_LAG, 0) is not None:
+                regroup_hidden(block_of(completed(step, REGROUP_LAG, 0)))
             if step < len(chunks):
                 regroup(step)
             if step + RAW_BUFS < LOADS:
                 load_weights(step + RAW_BUFS)
             if step < 2:
                 prepare_inputs(step)
-            if completed(step, REQUANTISE_LAG, 0) is not None:
-                quantise_hidden(block_of(completed(step, REQUANTISE_LAG, 0)))
             if 0 <= step - QUANTISE_LAG < len(chunks):
                 quantise_weights(step - QUANTISE_LAG)
+            if completed(step, REQUANTISE_LAG, 0) is not None:
+                quantise_hidden(block_of(completed(step, REQUANTISE_LAG, 0)))
             if 0 <= step - MULTIPLY_LAG < len(chunks):
                 multiply(step - MULTIPLY_LAG)
             if completed(step, BIAS_LAG, 0) is not None:

@@ -30,9 +30,10 @@ NARROW_LOADS = 4
 CHUNK_WORDS = 2 * BLOCK_COLS
 
 RAW_BUFS = 10
-RUN = 4
+RUN = 8
+UNIT_RUN = 4
 
-VECTOR_CHUNKS = 11
+VECTOR_CHUNKS = 10
 
 QUANTISE_LAG = 1
 MULTIPLY_LAG = 2
@@ -130,16 +131,28 @@ def tile_matchingnet_pb_kernel(tc, p, q, W1, b1, W2, b2, out):
             layer, block, first_col, width, passes = chunks[chunk]
             grouped = grouped_pool.tile([P, CHUNK_WORDS * PACK], BF16, align_bytes=64)
             grouped_of[chunk] = grouped
-            order = "r (c i w t) -> r c w t i" if layer == 0 else "r (c w i t) -> r c w t i"
-            dst = grouped[:].rearrange(order, c=len(passes), i=RUN, t=PACK)
+            by_pass = grouped[:].rearrange("r (c x) -> r c x", c=len(passes))
             load_block, offset = divmod(first_col, BLOCK_COLS)
             for c, k_pass in enumerate(passes):
                 raw = raw_of[layer, k_pass, load_block][:, :, offset : offset + width]
-                src = raw.rearrange("r t (w i) -> r w t i", i=RUN)
-                if chunk < VECTOR_CHUNKS and c == 0:
-                    nc.vector.tensor_copy(out=dst[:, c], in_=src)
+                words = by_pass[:, c]
+                on_vector = chunk < VECTOR_CHUNKS and c == 0
+                if layer == 0 and on_vector:
+                    nc.vector.tensor_copy(
+                        out=words.rearrange("r (b m h t) -> r m t h b", b=PACK, h=RUN // PACK, t=PACK),
+                        in_=raw.rearrange("r t (m h b) -> r m t h b", b=PACK, h=RUN // PACK),
+                    )
+                elif layer == 0:
+                    nc.scalar.copy(
+                        out=words.rearrange("r (b m t) -> r m t b", b=PACK, t=PACK),
+                        in_=raw.rearrange("r t (m b) -> r m t b", b=UNIT_RUN),
+                    )
                 else:
-                    nc.scalar.copy(out=dst[:, c], in_=src)
+                    copy = nc.vector.tensor_copy if on_vector else nc.scalar.copy
+                    copy(
+                        out=words.rearrange("r (w i t) -> r w t i", i=RUN, t=PACK),
+                        in_=raw.rearrange("r t (w i) -> r w t i", i=RUN),
+                    )
 
         def quantise_weights(chunk):
             codes = weight_pool.tile([P, CHUNK_WORDS], U32, align_bytes=64)

@@ -82,6 +82,7 @@ def tile_matchingnet_pb_kernel(tc, p, q, W1, b1, W2, b2, out):
         rounded_of = {}
         hidden_of = {}
         result_of = {}
+        x_tile_of = {}
 
         x_codes = keep.tile([P, PASSES, BATCH], U32, align_bytes=64)
         x_scales = keep.tile([P, PASSES, BATCH], U8, align_bytes=64)
@@ -119,13 +120,12 @@ def tile_matchingnet_pb_kernel(tc, p, q, W1, b1, W2, b2, out):
             for n in range(LOAD_COLS // BLOCK_COLS):
                 raw_of[layer, k_pass, 2 * part + n] = raw[:, :, n * BLOCK_COLS : (n + 1) * BLOCK_COLS]
 
-        def load_inputs(half):
-            words = slice(half * WIDTH // 4, (half + 1) * WIDTH // 4)
-            for name, table in (("p", p), ("q", q)):
-                rows = keep.tile([P, SAMPLE_TILES, WIDTH // 4], BF16, name="%s_rows%d" % (name, half))
+        def load_inputs(pair):
+            rows = raw_pool.tile([P, 2, 2, WIDTH // 2], BF16, tag="raw")
+            for e, table in enumerate((p, q)):
                 by_sample = table.rearrange("(r s) i j -> r s (i j)", s=SAMPLE_TILES)
-                nc.sync.dma_start(out=rows[:], in_=by_sample[:, :, words])
-                x_rows_of[name, half] = rows
+                nc.sync.dma_start(out=rows[:, e], in_=by_sample[:, 2 * pair : 2 * pair + 2, :])
+            x_rows_of[pair] = rows
 
         def regroup(chunk):
             layer, block, first_col, width, passes = chunks[chunk]
@@ -197,32 +197,32 @@ def tile_matchingnet_pb_kernel(tc, p, q, W1, b1, W2, b2, out):
                         stop=(k_pass == PASSES - 1),
                     )
 
-        def prepare_inputs(half):
-            words_of_table = [x_rows_of[name, half][:].bitcast(F32) for name in ("p", "q")]
-            grouped_x = {}
-            for c in range(2):
-                k_pass = 2 * half + c
-                x_tile = hidden_pool.tile([P, BATCH * PACK], BF16, tag="x", align_bytes=64)
-                x_words = x_tile[:].bitcast(F32).rearrange("r (n e) -> r n e", e=2)
-                for pair in range(SAMPLE_TILES // 2):
-                    bank = psum.tile([P, 2, 2 * P], F32, tag="bank")
-                    for e in range(2):
-                        for s in range(2):
-                            nc.tensor.transpose(
-                                bank[:, e, s * P : (s + 1) * P],
-                                words_of_table[e][:, 2 * pair + s, c * P : (c + 1) * P],
-                                ident_f32[:],
-                            )
-                    nc.scalar.copy(
-                        out=x_words[:, pair * 2 * P : (pair + 1) * 2 * P, :],
-                        in_=bank[:].rearrange("r e n -> r n e"),
+        def prepare_inputs(pair):
+            words = x_rows_of[pair][:].rearrange("r e s f -> r (e s f)").bitcast(F32)
+            sample_words = WIDTH // 4
+            for k_pass in range(PASSES):
+                if pair == 0:
+                    x_tile_of[k_pass] = hidden_pool.tile(
+                        [P, BATCH * PACK], BF16, tag="x", bufs=PASSES, align_bytes=64, name="x_tile"
                     )
-                grouped_x[k_pass] = x_tile
-            for k_pass in (2 * half, 2 * half + 1):
+                x_words = x_tile_of[k_pass][:].bitcast(F32).rearrange("r (n e) -> r n e", e=2)
+                bank = psum.tile([P, 2, 2 * P], F32, tag="bank")
+                for e in range(2):
+                    for s in range(2):
+                        first = (2 * e + s) * sample_words + k_pass * P
+                        nc.tensor.transpose(
+                            bank[:, e, s * P : (s + 1) * P], words[:, first : first + P], ident_f32[:]
+                        )
+                nc.scalar.copy(
+                    out=x_words[:, pair * 2 * P : (pair + 1) * 2 * P, :], in_=bank[:].rearrange("r e n -> r n e")
+                )
+
+        def quantise_inputs():
+            for k_pass in range(PASSES):
                 nc.vector.quantize_mx(
                     out=x_codes[:, k_pass, :].bitcast(FP8X4),
                     scales=x_scales[:, k_pass, :],
-                    in_=grouped_x[k_pass][:],
+                    in_=x_tile_of[k_pass][:],
                 )
 
         def add_hidden_bias(block):
@@ -313,6 +313,8 @@ def tile_matchingnet_pb_kernel(tc, p, q, W1, b1, W2, b2, out):
                 load_weights(step + RAW_BUFS)
             if step < 2:
                 prepare_inputs(step)
+            if step == 1:
+                quantise_inputs()
             if 0 <= step - QUANTISE_LAG < len(chunks):
                 quantise_weights(step - QUANTISE_LAG)
             if completed(step, REQUANTISE_LAG, 0) is not None:

@@ -43,6 +43,8 @@ REGROUP_LAG = 4
 REQUANTISE_LAG = 4
 FINISH_LAG = 2
 
+TURNED_CHUNKS = (14,)
+
 FLOPS = 2 * 2 * BATCH * WIDTH * WIDTH
 
 
@@ -82,6 +84,7 @@ def tile_matchingnet_pb_kernel(tc, p, q, W1, b1, W2, b2, out):
         rounded_of = {}
         hidden_of = {}
         result_of = {}
+        turned_of = {}
         x_tile_of = {}
 
         x_codes = keep.tile([P, PASSES, BATCH], U32, align_bytes=64)
@@ -90,6 +93,8 @@ def tile_matchingnet_pb_kernel(tc, p, q, W1, b1, W2, b2, out):
         h_scales = keep.tile([P, PASSES, BATCH], U8, align_bytes=64)
         b1_cols = keep.tile([P, WIDTH // BLOCK_COLS, PACK], BF16)
         b2_all = keep.tile([P, WIDTH], BF16)
+        b2_cols = keep.tile([P, LAST_COLS // P], F32)
+        ident_bf16 = keep.tile([P, P], BF16)
         ident_f32 = keep.tile([P, P], F32)
         one = keep.tile([P, 1], F32)
         loaded = keep.tile([P, 1], F32)
@@ -170,11 +175,26 @@ def tile_matchingnet_pb_kernel(tc, p, q, W1, b1, W2, b2, out):
         def multiply(chunk):
             layer, block, first_col, width, passes = chunks[chunk]
             if passes[0] == 0:
+                count = width // P if chunk in TURNED_CHUNKS else BANKS
                 banks_of[layer, block] = [
-                    psum.tile([P, BLOCK_COLS], F32, tag="bank", name="acc%d" % b) for b in range(BANKS)
+                    psum.tile([P, BLOCK_COLS], F32, tag="bank", name="acc%d" % b) for b in range(count)
                 ]
             codes = codes_of[chunk]
             scales = scales_of[chunk]
+            if chunk in TURNED_CHUNKS:
+                for b in range(width // P):
+                    for c, k_pass in enumerate(passes):
+                        columns = slice(c * width + b * P, c * width + (b + 1) * P)
+                        nc.tensor.matmul_mx(
+                            out=banks_of[layer, block][b][:],
+                            lhsT=codes[:, columns].bitcast(FP8X4),
+                            lhsT_scale=scales[:, columns],
+                            rhs=h_codes[:, k_pass, :].bitcast(FP8X4),
+                            rhs_scale=h_scales[:, k_pass, :],
+                            start=(k_pass == 0),
+                            stop=(k_pass == PASSES - 1),
+                        )
+                return
             for b in range(BANKS):
                 tile_cols = slice(b * P, (b + 1) * P)
                 for c, k_pass in enumerate(passes):
@@ -283,9 +303,56 @@ def tile_matchingnet_pb_kernel(tc, p, q, W1, b1, W2, b2, out):
                 out=rows[:, first_tile : first_tile + 2, first_col : first_col + width], in_=result[:]
             )
 
+        def prepare_output_bias(chunk):
+            layer, block, first_col, width, passes = chunks[chunk]
+            bank = psum.tile([P, width // P, P], BF16, tag="bank")
+            for b in range(width // P):
+                here = slice(first_col + b * P, first_col + (b + 1) * P)
+                nc.tensor.transpose(bank[:, b, :], b2_all[:, here], ident_bf16[:])
+            nc.scalar.copy(out=b2_cols[:].rearrange("r (b o) -> r b o", o=1), in_=bank[:, :, :1])
+
+        def add_turned_bias(chunk):
+            layer, block, first_col, width, passes = chunks[chunk]
+            turned = result_pool.tile([P, width // P, BATCH], F32, tag="result")
+            for b in range(width // P):
+                nc.scalar.activation(
+                    out=turned[:, b, :],
+                    in_=banks_of[1, block][b][:],
+                    func=ACT.Identity,
+                    bias=b2_cols[:, b : b + 1],
+                    scale=1.0,
+                )
+            turned_of[chunk] = turned
+
+        def leaky_turned(chunk):
+            layer, block, first_col, width, passes = chunks[chunk]
+            for b in range(width // P):
+                values = turned_of[chunk][:, b, :]
+                nc.vector.scalar_tensor_tensor(
+                    out=values, in0=values, scalar=SLOPE, in1=values, op0=ALU.mult, op1=ALU.max
+                )
+
+        def turn_back(chunk):
+            layer, block, first_col, width, passes = chunks[chunk]
+            rows = out.rearrange("(r s) j -> r s j", s=SAMPLE_TILES)
+            for first_tile in (0, 2):
+                bank = psum.tile([P, 2, width], F32, tag="bank")
+                for s in range(2):
+                    samples = slice((first_tile + s) * P, (first_tile + s + 1) * P)
+                    for b in range(width // P):
+                        nc.tensor.transpose(
+                            bank[:, s, b * P : (b + 1) * P], turned_of[chunk][:, b, samples], ident_f32[:]
+                        )
+                result = result_pool.tile([P, 2, width], F32, tag="result")
+                nc.scalar.copy(out=result[:], in_=bank[:])
+                nc.sync.dma_start(
+                    out=rows[:, first_tile : first_tile + 2, first_col : first_col + width], in_=result[:]
+                )
+
         nc.vector.memset(one[:], 1.0)
         nc.scalar.activation(out=loaded[:], in_=one[:], func=ACT.Identity)
         make_identity(nc, ident_f32[:])
+        make_identity(nc, ident_bf16[:])
         nc.scalar.dma_start(out=b1_cols[:], in_=b1.rearrange("(b p t) -> p b t", p=P, t=PACK))
         load_weights(0)
         load_inputs(0)
@@ -326,8 +393,17 @@ def tile_matchingnet_pb_kernel(tc, p, q, W1, b1, W2, b2, out):
             if completed(step, LEAKY_LAG, 0) is not None:
                 leaky_hidden(block_of(completed(step, LEAKY_LAG, 0)))
             for half_lag, first_tile in ((0, 0), (1, 2)):
-                if completed(step, FINISH_LAG + half_lag, 1) is not None:
-                    add_output_bias(completed(step, FINISH_LAG + half_lag, 1), first_tile)
+                chunk = completed(step, FINISH_LAG + half_lag, 1)
+                if chunk is not None and chunk not in TURNED_CHUNKS:
+                    add_output_bias(chunk, first_tile)
             for half_lag, first_tile in ((0, 0), (1, 2)):
-                if completed(step, FINISH_LAG + half_lag + 1, 1) is not None:
-                    leaky_output(completed(step, FINISH_LAG + half_lag + 1, 1), first_tile)
+                chunk = completed(step, FINISH_LAG + half_lag + 1, 1)
+                if chunk is not None and chunk not in TURNED_CHUNKS:
+                    leaky_output(chunk, first_tile)
+            if step - FINISH_LAG in TURNED_CHUNKS:
+                add_turned_bias(step - FINISH_LAG)
+                leaky_turned(step - FINISH_LAG)
+            if step - FINISH_LAG - 1 in TURNED_CHUNKS:
+                turn_back(step - FINISH_LAG - 1)
+            if step in TURNED_CHUNKS:
+                prepare_output_bias(step)

from contextlib import ExitStack

import concourse.mybir as mybir
from concourse.masks import make_identity

F32 = mybir.dt.float32
BF16 = mybir.dt.bfloat16
U32 = mybir.dt.uint32
U8 = mybir.dt.uint8
FP8X4 = mybir.dt.float8_e4m3fn_x4
ALU = mybir.AluOpType
ACT = mybir.ActivationFunctionType

P = 128
PACK = 4
K_PASS = P * PACK
BATCH = 512
WIDTH = 2048
SLOPE = 0.01
PASSES = WIDTH // K_PASS
SAMPLE_TILES = BATCH // P

BLOCK_COLS = 512
LAST_COLS = 256
BANKS = 4
LOAD_COLS = 2 * BLOCK_COLS
LAYER_LOADS = PASSES * (WIDTH // LOAD_COLS)
LOADS = 2 * LAYER_LOADS
NARROW_LOADS = 4
CHUNK_WORDS = 2 * BLOCK_COLS

RAW_BUFS = 10
RUN = 8
UNIT_RUN = 4

VECTOR_CHUNKS = 10

QUANTISE_LAG = 1
MULTIPLY_LAG = 2
BIAS_LAG = 2
LEAKY_LAG = 3
REGROUP_LAG = 4
REQUANTISE_LAG = 4
FINISH_LAG = 2

TURNED_CHUNKS = (14,)

FLOPS = 2 * 2 * BATCH * WIDTH * WIDTH


def plan_chunks():
    chunks = []
    for layer in range(2):
        for block in range(WIDTH // BLOCK_COLS):
            start = block * BLOCK_COLS
            if (layer, block) == (1, WIDTH // BLOCK_COLS - 1):
                for half in range(2):
                    chunks.append((1, block + half, start + half * LAST_COLS, LAST_COLS, range(4)))
            else:
                chunks.append((layer, block, start, BLOCK_COLS, range(0, 2)))
                chunks.append((layer, block, start, BLOCK_COLS, range(2, 4)))
    return chunks


def tile_matchingnet_pb_kernel(tc, p, q, W1, b1, W2, b2, out):
    nc = tc.nc
    chunks = plan_chunks()
    with ExitStack() as ctx:
        keep = ctx.enter_context(tc.tile_pool(name="keep", bufs=1))
        raw_pool = ctx.enter_context(tc.tile_pool(name="raw", bufs=RAW_BUFS))
        grouped_pool = ctx.enter_context(tc.tile_pool(name="grouped", bufs=4))
        weight_pool = ctx.enter_context(tc.tile_pool(name="weight", bufs=4))
        hidden_pool = ctx.enter_context(tc.tile_pool(name="hidden", bufs=2))
        result_pool = ctx.enter_context(tc.tile_pool(name="result", bufs=6))
        psum = ctx.enter_context(tc.psum_pool(name="psum", bufs=8))

        x_rows_of = {}
        raw_of = {}
        grouped_of = {}
        codes_of = {}
        scales_of = {}
        banks_of = {}
        biased_of = {}
        rounded_of = {}
        hidden_of = {}
        result_of = {}
        turned_of = {}
        x_tile_of = {}

        x_codes = keep.tile([P, PASSES, BATCH], U32, align_bytes=64)
        x_scales = keep.tile([P, PASSES, BATCH], U8, align_bytes=64)
        h_codes = keep.tile([P, PASSES, BATCH], U32, align_bytes=64)
        h_scales = keep.tile([P, PASSES, BATCH], U8, align_bytes=64)
        b1_cols = keep.tile([P, WIDTH // BLOCK_COLS, PACK], BF16)
        b2_all = keep.tile([P, WIDTH], BF16)
        b2_cols = keep.tile([P, LAST_COLS // P], F32)
        ident_bf16 = keep.tile([P, P], BF16)
        ident_f32 = keep.tile([P, P], F32)
        one = keep.tile([P, 1], F32)
        loaded = keep.tile([P, 1], F32)

        def load_weights(load):
            layer, rest = divmod(load, LAYER_LOADS)
            if load < NARROW_LOADS:
                block, half = divmod(load, 2)
                rows = slice(2 * half * K_PASS, 2 * (half + 1) * K_PASS)
                cols = slice(block * BLOCK_COLS, (block + 1) * BLOCK_COLS)
                raw = raw_pool.tile([P, 2, PACK, BLOCK_COLS], BF16, tag="raw")
                by_table = W1[rows, cols].rearrange("(c r u e) w -> c e r u w", c=2, u=2, e=2)
                for c in range(2):
                    for e in range(2):
                        nc.sync.dma_start(out=raw[:, c, 2 * e : 2 * e + 2, :], in_=by_table[c, e])
                    raw_of[0, 2 * half + c, block] = raw[:, c]
                return
            part, k_pass = divmod(rest, PASSES)
            rows = slice(k_pass * K_PASS, (k_pass + 1) * K_PASS)
            cols = slice(part * LOAD_COLS, (part + 1) * LOAD_COLS)
            raw = raw_pool.tile([P, PACK, LOAD_COLS], BF16, tag="raw")
            if layer == 0:
                by_table = W1[rows, cols].rearrange("(r u e) w -> e r u w", u=2, e=2)
                for e in range(2):
                    nc.sync.dma_start(out=raw[:, 2 * e : 2 * e + 2, :], in_=by_table[e])
            else:
                nc.sync.dma_start(out=raw[:], in_=W2[rows, cols].rearrange("(r t) w -> r t w", r=P))
            for n in range(LOAD_COLS // BLOCK_COLS):
                raw_of[layer, k_pass, 2 * part + n] = raw[:, :, n * BLOCK_COLS : (n + 1) * BLOCK_COLS]

        def load_inputs(pair):
            rows = raw_pool.tile([P, 2, 2, WIDTH // 2], BF16, tag="raw")
            for e, table in enumerate((p, q)):
                by_sample = table.rearrange("(r s) i j -> r s (i j)", s=SAMPLE_TILES)
                nc.sync.dma_start(out=rows[:, e], in_=by_sample[:, 2 * pair : 2 * pair + 2, :])
            x_rows_of[pair] = rows

        def regroup(chunk):
            layer, block, first_col, width, passes = chunks[chunk]
            grouped = grouped_pool.tile([P, CHUNK_WORDS * PACK], BF16, align_bytes=64)
            grouped_of[chunk] = grouped
            by_pass = grouped[:].rearrange("r (c x) -> r c x", c=len(passes))
            load_block, offset = divmod(first_col, BLOCK_COLS)
            for c, k_pass in enumerate(passes):
                raw = raw_of[layer, k_pass, load_block][:, :, offset : offset + width]
                words = by_pass[:, c]
                on_vector = chunk < VECTOR_CHUNKS and c == 0
                if layer == 0 and on_vector:
                    nc.vector.tensor_copy(
                        out=words.rearrange("r (b m h t) -> r m t h b", b=PACK, h=RUN // PACK, t=PACK),
                        in_=raw.rearrange("r t (m h b) -> r m t h b", b=PACK, h=RUN // PACK),
                    )
                elif layer == 0:
                    nc.scalar.copy(
                        out=words.rearrange("r (b m t) -> r m t b", b=PACK, t=PACK),
                        in_=raw.rearrange("r t (m b) -> r m t b", b=UNIT_RUN),
                    )
                else:
                    copy = nc.vector.tensor_copy if on_vector else nc.scalar.copy
                    copy(
                        out=words.rearrange("r (w i t) -> r w t i", i=RUN, t=PACK),
                        in_=raw.rearrange("r t (w i) -> r w t i", i=RUN),
                    )

        def quantise_weights(chunk):
            codes = weight_pool.tile([P, CHUNK_WORDS], U32, align_bytes=64)
            scales = weight_pool.tile([P, CHUNK_WORDS], U8, align_bytes=64)
            for half in range(2):
                words = slice(half * CHUNK_WORDS // 2, (half + 1) * CHUNK_WORDS // 2)
                nc.vector.quantize_mx(
                    out=codes[:, words].bitcast(FP8X4),
                    scales=scales[:, words],
                    in_=grouped_of[chunk][:, PACK * words.start : PACK * words.stop],
                )
            codes_of[chunk] = codes
            scales_of[chunk] = scales

        def multiply(chunk):
            layer, block, first_col, width, passes = chunks[chunk]
            if passes[0] == 0:
                count = width // P if chunk in TURNED_CHUNKS else BANKS
                banks_of[layer, block] = [
                    psum.tile([P, BLOCK_COLS], F32, tag="bank", name="acc%d" % b) for b in range(count)
                ]
            codes = codes_of[chunk]
            scales = scales_of[chunk]
            if chunk in TURNED_CHUNKS:
                for b in range(width // P):
                    for c, k_pass in enumerate(passes):
                        columns = slice(c * width + b * P, c * width + (b + 1) * P)
                        nc.tensor.matmul_mx(
                            out=banks_of[layer, block][b][:],
                            lhsT=codes[:, columns].bitcast(FP8X4),
                            lhsT_scale=scales[:, columns],
                            rhs=h_codes[:, k_pass, :].bitcast(FP8X4),
                            rhs_scale=h_scales[:, k_pass, :],
                            start=(k_pass == 0),
                            stop=(k_pass == PASSES - 1),
                        )
                return
            for b in range(BANKS):
                tile_cols = slice(b * P, (b + 1) * P)
                for c, k_pass in enumerate(passes):
                    first = c * width
                    if layer == 0:
                        units = slice(first + b * P, first + (b + 1) * P)
                        lhsT, lhsT_scale = codes[:, units], scales[:, units]
                        rhs, rhs_scale = x_codes[:, k_pass, :], x_scales[:, k_pass, :]
                    else:
                        lhsT, lhsT_scale = h_codes[:, k_pass, tile_cols], h_scales[:, k_pass, tile_cols]
                        columns = slice(first, first + width)
                        rhs, rhs_scale = codes[:, columns], scales[:, columns]
                    nc.tensor.matmul_mx(
                        out=banks_of[layer, block][b][:, : BATCH if layer == 0 else width],
                        lhsT=lhsT.bitcast(FP8X4),
                        lhsT_scale=lhsT_scale,
                        rhs=rhs.bitcast(FP8X4),
                        rhs_scale=rhs_scale,
                        start=(k_pass == 0),
                        stop=(k_pass == PASSES - 1),
                    )

        def prepare_inputs(pair):
            words = x_rows_of[pair][:].rearrange("r e s f -> r (e s f)").bitcast(F32)
            sample_words = WIDTH // 4
            for k_pass in range(PASSES):
                if pair == 0:
                    x_tile_of[k_pass] = hidden_pool.tile(
                        [P, BATCH * PACK], BF16, tag="x", bufs=PASSES, align_bytes=64, name="x_tile"
                    )
                x_words = x_tile_of[k_pass][:].bitcast(F32).rearrange("r (n e) -> r n e", e=2)
                bank = psum.tile([P, 2, 2 * P], F32, tag="bank")
                for e in range(2):
                    for s in range(2):
                        first = (2 * e + s) * sample_words + k_pass * P
                        nc.tensor.transpose(
                            bank[:, e, s * P : (s + 1) * P], words[:, first : first + P], ident_f32[:]
                        )
                nc.scalar.copy(
                    out=x_words[:, pair * 2 * P : (pair + 1) * 2 * P, :], in_=bank[:].rearrange("r e n -> r n e")
                )

        def quantise_inputs():
            for k_pass in range(PASSES):
                nc.vector.quantize_mx(
                    out=x_codes[:, k_pass, :].bitcast(FP8X4),
                    scales=x_scales[:, k_pass, :],
                    in_=x_tile_of[k_pass][:],
                )

        def add_hidden_bias(block):
            biased = hidden_pool.tile([P, PACK, BATCH], F32)
            for t in range(PACK):
                nc.scalar.activation(
                    out=biased[:, t, :],
                    in_=banks_of[0, block][t][:],
                    func=ACT.Identity,
                    bias=b1_cols[:, block, t : t + 1],
                    scale=1.0,
                )
            biased_of[block] = biased

        def leaky_hidden(block):
            rounded = hidden_pool.tile([P, PACK, BATCH], BF16)
            biased = biased_of[block]
            nc.vector.scalar_tensor_tensor(
                out=rounded[:], in0=biased[:], scalar=SLOPE, in1=biased[:], op0=ALU.mult, op1=ALU.max
            )
            rounded_of[block] = rounded

        def regroup_hidden(block):
            hidden = hidden_pool.tile([P, BATCH * PACK], BF16, align_bytes=64)
            nc.vector.tensor_copy(
                out=hidden[:].rearrange("r (n i t) -> r n t i", i=RUN, t=PACK),
                in_=rounded_of[block][:].rearrange("r t (n i) -> r n t i", i=RUN),
            )
            hidden_of[block] = hidden

        def quantise_hidden(block):
            nc.vector.quantize_mx(
                out=h_codes[:, block, :].bitcast(FP8X4),
                scales=h_scales[:, block, :],
                in_=hidden_of[block][:],
            )

        def add_output_bias(chunk, first_tile):
            layer, block, first_col, width, passes = chunks[chunk]
            result = result_pool.tile([P, 2, width], F32, tag="result")
            for s in range(2):
                nc.vector.tensor_tensor(
                    out=result[:, s, :],
                    in0=banks_of[1, block][first_tile + s][:, :width],
                    in1=b2_all[:, first_col : first_col + width],
                    op=ALU.add,
                )
            result_of[chunk, first_tile] = result

        def leaky_output(chunk, first_tile):
            layer, block, first_col, width, passes = chunks[chunk]
            result = result_of[chunk, first_tile]
            nc.vector.scalar_tensor_tensor(
                out=result[:], in0=result[:], scalar=SLOPE, in1=result[:], op0=ALU.mult, op1=ALU.max
            )
            rows = out.rearrange("(r s) j -> r s j", s=SAMPLE_TILES)
            nc.sync.dma_start(
                out=rows[:, first_tile : first_tile + 2, first_col : first_col + width], in_=result[:]
            )

        def prepare_output_bias(chunk):
            layer, block, first_col, width, passes = chunks[chunk]
            bank = psum.tile([P, width // P, P], BF16, tag="bank")
            for b in range(width // P):
                here = slice(first_col + b * P, first_col + (b + 1) * P)
                nc.tensor.transpose(bank[:, b, :], b2_all[:, here], ident_bf16[:])
            nc.scalar.copy(out=b2_cols[:].rearrange("r (b o) -> r b o", o=1), in_=bank[:, :, :1])

        def add_turned_bias(chunk):
            layer, block, first_col, width, passes = chunks[chunk]
            turned = result_pool.tile([P, width // P, BATCH], F32, tag="result")
            for b in range(width // P):
                nc.scalar.activation(
                    out=turned[:, b, :],
                    in_=banks_of[1, block][b][:],
                    func=ACT.Identity,
                    bias=b2_cols[:, b : b + 1],
                    scale=1.0,
                )
            turned_of[chunk] = turned

        def leaky_turned(chunk):
            layer, block, first_col, width, passes = chunks[chunk]
            for b in range(width // P):
                values = turned_of[chunk][:, b, :]
                nc.vector.scalar_tensor_tensor(
                    out=values, in0=values, scalar=SLOPE, in1=values, op0=ALU.mult, op1=ALU.max
                )

        def turn_back(chunk):
            layer, block, first_col, width, passes = chunks[chunk]
            rows = out.rearrange("(r s) j -> r s j", s=SAMPLE_TILES)
            for first_tile in (0, 2):
                bank = psum.tile([P, 2, width], F32, tag="bank")
                for s in range(2):
                    samples = slice((first_tile + s) * P, (first_tile + s + 1) * P)
                    for b in range(width // P):
                        nc.tensor.transpose(
                            bank[:, s, b * P : (b + 1) * P], turned_of[chunk][:, b, samples], ident_f32[:]
                        )
                result = result_pool.tile([P, 2, width], F32, tag="result")
                nc.scalar.copy(out=result[:], in_=bank[:])
                nc.sync.dma_start(
                    out=rows[:, first_tile : first_tile + 2, first_col : first_col + width], in_=result[:]
                )

        nc.vector.memset(one[:], 1.0)
        nc.scalar.activation(out=loaded[:], in_=one[:], func=ACT.Identity)
        make_identity(nc, ident_f32[:])
        make_identity(nc, ident_bf16[:])
        nc.scalar.dma_start(out=b1_cols[:], in_=b1.rearrange("(b p t) -> p b t", p=P, t=PACK))
        load_weights(0)
        load_inputs(0)
        load_weights(1)
        load_inputs(1)
        for load in range(2, RAW_BUFS):
            load_weights(load)
        nc.sync.dma_start(out=b2_all[:], in_=b2.partition_broadcast(P))

        def completed(step, lag, layer):
            chunk = step - lag
            if 0 <= chunk < len(chunks) and chunks[chunk][0] == layer and chunks[chunk][4][-1] == PASSES - 1:
                return chunk
            return None

        def block_of(chunk):
            return chunks[chunk][1]

        for step in range(len(chunks) + FINISH_LAG + 2):
            if completed(step, REGROUP_LAG, 0) is not None:
                regroup_hidden(block_of(completed(step, REGROUP_LAG, 0)))
            if step < len(chunks):
                regroup(step)
            if step + RAW_BUFS < LOADS:
                load_weights(step + RAW_BUFS)
            if step < 2:
                prepare_inputs(step)
            if step == 1:
                quantise_inputs()
            if 0 <= step - QUANTISE_LAG < len(chunks):
                quantise_weights(step - QUANTISE_LAG)
            if completed(step, REQUANTISE_LAG, 0) is not None:
                quantise_hidden(block_of(completed(step, REQUANTISE_LAG, 0)))
            if 0 <= step - MULTIPLY_LAG < len(chunks):
                multiply(step - MULTIPLY_LAG)
            if completed(step, BIAS_LAG, 0) is not None:
                add_hidden_bias(block_of(completed(step, BIAS_LAG, 0)))
            if completed(step, LEAKY_LAG, 0) is not None:
                leaky_hidden(block_of(completed(step, LEAKY_LAG, 0)))
            for half_lag, first_tile in ((0, 0), (1, 2)):
                chunk = completed(step, FINISH_LAG + half_lag, 1)
                if chunk is not None and chunk not in TURNED_CHUNKS:
                    add_output_bias(chunk, first_tile)
            for half_lag, first_tile in ((0, 0), (1, 2)):
                chunk = completed(step, FINISH_LAG + half_lag + 1, 1)
                if chunk is not None and chunk not in TURNED_CHUNKS:
                    leaky_output(chunk, first_tile)
            if step - FINISH_LAG in TURNED_CHUNKS:
                add_turned_bias(step - FINISH_LAG)
                leaky_turned(step - FINISH_LAG)
            if step - FINISH_LAG - 1 in TURNED_CHUNKS:
                turn_back(step - FINISH_LAG - 1)
            if step in TURNED_CHUNKS:
                prepare_output_bias(step)
